import numpy as np
import ml_dtypes


def mxq(x, axis, fmt="e4m3"):
    dtype, down = {"e4m3": (ml_dtypes.float8_e4m3fn, 7), "e5m2": (ml_dtypes.float8_e5m2, 14)}[fmt]
    v = np.moveaxis(np.asarray(x, np.float32).astype(ml_dtypes.bfloat16).astype(np.float64), axis, -1)
    blocks = v.reshape(v.shape[:-1] + (-1, 32))
    amax = np.abs(blocks).max(-1, keepdims=True)
    byte = np.maximum(np.where(amax > 0, np.frexp(amax)[1] - 1 + 127, 0) - down, 1)
    scale = np.exp2(byte - 127.0)
    codes = (blocks / scale).astype(np.float32).astype(dtype).astype(np.float64)
    return np.moveaxis((codes * scale).reshape(v.shape), -1, axis)


WIDE = False


def mx_kscale(k):
    if not WIDE:
        return np.ones(k)
    levels = np.array([10, -10, 5, -5, 0])
    a = np.random.permutation(np.resize(levels, k // 512 * 4)).reshape(k // 512, 4)
    idx = np.arange(k)
    return np.exp2(a[idx // 512, idx % 128 // 32])


BF16 = ml_dtypes.bfloat16


def bf(x):
    return np.asarray(x, np.float32).astype(BF16)


def f64(x):
    return np.asarray(x).astype(np.float64)


N, LMAX, CIN, COUT = 128, 3, 1024, 1024
NL = LMAX + 1
NM = NL * NL


def setup_inputs():
    s = mx_kscale(CIN)
    return {"x": bf(np.random.standard_normal((N, NM, CIN)) * s),
            "weights": bf(np.random.standard_normal((NL, CIN, COUT)) / np.sqrt(CIN) / s[:, None]),
            "path_weights": bf(1.0 + 0.3 * np.random.standard_normal(NL))}


def reference(x, weights, path_weights):
    x, weights, path_weights = f64(x), f64(weights), f64(path_weights)
    blocks = []
    for l in range(LMAX + 1):
        start = l * l
        end = start + (2 * l + 1)
        blk = mxq(x[:, start:end, :], 2, "e4m3") @ mxq(weights[l], 0, "e4m3")
        blocks.append(path_weights[l] * blk)
    return np.concatenate(blocks, axis=1)

@@ -1,0 +1,171 @@
+from contextlib import ExitStack
+
+import concourse.mybir as mybir
+from concourse.masks import make_identity
+
+F32 = mybir.dt.float32
+BF16 = mybir.dt.bfloat16
+U32 = mybir.dt.uint32
+U8 = mybir.dt.uint8
+FP8X4 = mybir.dt.float8_e4m3fn_x4
+COPY = mybir.ActivationFunctionType.Copy
+
+P = 128
+NM = 16
+CIN = 1024
+COUT = 1024
+FLOPS = 2 * P * NM * CIN * COUT
+DEGREE = (0, 1, 1, 1, 2, 2, 2, 2, 2, 3, 3, 3, 3, 3, 3, 3)
+
+
+def tile_linear_pa_kernel(tc, x, weights, path_weights, out):
+    nc = tc.nc
+    with ExitStack() as ctx:
+        const = ctx.enter_context(tc.tile_pool(name="const", bufs=1))
+        xraw = ctx.enter_context(tc.tile_pool(name="xraw", bufs=1))
+        wraw = ctx.enter_context(tc.tile_pool(name="wraw", bufs=1))
+        wgp = ctx.enter_context(tc.tile_pool(name="wgp", bufs=3))
+        wcp = ctx.enter_context(tc.tile_pool(name="wcp", bufs=4))
+        xgp = ctx.enter_context(tc.tile_pool(name="xgp", bufs=2))
+        xcp = ctx.enter_context(tc.tile_pool(name="xcp", bufs=1))
+        outp = ctx.enter_context(tc.tile_pool(name="outp", bufs=6))
+        psum_t = ctx.enter_context(tc.psum_pool(name="psum_t", bufs=3))
+        psum_a = ctx.enter_context(tc.psum_pool(name="psum_a", bufs=5))
+
+        ident = const.tile([P, P], F32)
+        make_identity(nc, ident[:])
+        ones = const.tile([P, P], BF16)
+        nc.vector.memset(ones[:], 1.0)
+        pw_row = const.tile([P, 32], BF16)
+        nc.vector.memset(pw_row[:], 0.0)
+        nc.scalar.dma_start(out=pw_row[0:1, 0:4], in_=path_weights.unsqueeze(0))
+
+        xr = {}
+        wr = {}
+
+        def load_x(grp):
+            t = xraw.tile([P, 4 * CIN], BF16, name="xr%d" % grp)
+            nc.sync.dma_start(out=t[:], in_=x[:, 4 * grp:4 * grp + 4, :].rearrange("n m k -> n (m k)"))
+            xr[grp] = t
+
+        def load_w(l, g):
+            t = wraw.tile([P, 4 * COUT], BF16, name="wr%d%d" % (l, g))
+            nc.sync.dma_start(
+                out=t[:].rearrange("p (u f) -> p u f", u=2),
+                in_=weights[l, 512 * g:512 * g + 512, :].rearrange("(u p e) n -> p u (e n)", u=2, p=P, e=2),
+            )
+            wr[(l, g)] = t
+
+        load_w(3, 0)
+        load_x(3)
+        load_w(3, 1)
+        load_x(2)
+        load_w(2, 0)
+        load_w(2, 1)
+        load_x(1)
+        load_w(1, 0)
+        load_w(1, 1)
+        load_x(0)
+        load_w(0, 0)
+        load_w(0, 1)
+
+        pw_ps = psum_t.tile([P, 512], F32, tag="xt")
+        nc.tensor.matmul(out=pw_ps[:, 0:32], lhsT=ones[:], rhs=pw_row[:], start=True, stop=True)
+        pw = const.tile([P, 4], F32)
+        nc.vector.tensor_copy(out=pw[:], in_=pw_ps[:, 0:4])
+
+        xg = {}
+        xc = {}
+        xs = {}
+        wc = {}
+        ws = {}
+
+        def transpose_x(grp):
+            words = xr[grp][:].bitcast(F32)
+            g_t = xgp.tile([P, 4 * CIN], BF16, name="xg%d" % grp, tag="xg", align_bytes=64)
+            g_w = g_t[:].bitcast(F32)
+            for r in range(4):
+                xt = psum_t.tile([P, 512], F32, tag="xt")
+                for j in range(4):
+                    c0 = 512 * r + 128 * j
+                    nc.tensor.transpose(xt[:, 128 * j:128 * j + 128], words[:, c0:c0 + 128], ident[:])
+                nc.scalar.copy(
+                    out=g_w[:, 512 * r:512 * r + 512].rearrange("p (g n u) -> p g n u", g=2, u=2),
+                    in_=xt[:].rearrange("p (g u n) -> p g n u", g=2, u=2),
+                )
+            xg[grp] = g_t
+
+        def quantise_x(grp):
+            c_t = xcp.tile([P, CIN], U32, name="xc%d" % grp, align_bytes=64)
+            s_t = xcp.tile([P, CIN], U8, name="xs%d" % grp, align_bytes=64)
+            nc.vector.quantize_mx(out=c_t[:].bitcast(FP8X4), scales=s_t[:], in_=xg[grp][:])
+            xc[grp] = c_t
+            xs[grp] = s_t
+
+        def quantise_w(l, g):
+            g_t = wgp.tile([P, 4 * COUT], BF16, name="wg%d%d" % (l, g), tag="wg", align_bytes=64)
+            nc.vector.tensor_copy(
+                out=g_t[:].rearrange("p (c i t) -> p c t i", i=4, t=4),
+                in_=wr[(l, g)][:].rearrange("p (t c i) -> p c t i", t=4, i=4),
+            )
+            c_t = wcp.tile([P, COUT], U32, name="wc%d%d" % (l, g), tag="wc", align_bytes=64)
+            s_t = wcp.tile([P, COUT], U8, name="ws%d%d" % (l, g), tag="ws", align_bytes=64)
+            nc.vector.quantize_mx(out=c_t[:].bitcast(FP8X4), scales=s_t[:], in_=g_t[:])
+            wc[(l, g)] = c_t
+            ws[(l, g)] = s_t
+
+        def multiply_row(m, o_ap):
+            l = DEGREE[m]
+            grp = m // 4
+            r = m % 4
+            for h in range(2):
+                acc = psum_a.tile([P, 512], F32, tag="acc")
+                for g in range(2):
+                    s0 = (2 * r + g) * P
+                    nc.tensor.matmul_mx(
+                        out=acc[:],
+                        lhsT=xc[grp][:, s0:s0 + P].bitcast(FP8X4),
+                        lhsT_scale=xs[grp][:, s0:s0 + P],
+                        rhs=wc[(l, g)][:, 512 * h:512 * h + 512].bitcast(FP8X4),
+                        rhs_scale=ws[(l, g)][:, 512 * h:512 * h + 512],
+                        start=(g == 0),
+                        stop=(g == 1),
+                    )
+                nc.scalar.activation(out=o_ap[:, 512 * h:512 * h + 512], in_=acc[:], func=COPY, scale=pw[:, l:l + 1])
+
+        state = {}
+
+        def rows(ms):
+            for m in ms:
+                if m >= 2:
+                    if m % 2 == 1:
+                        state["ot"] = outp.tile([P, 2 * COUT], F32, name="ot%d" % m, tag="ot")
+                    o_t = state["ot"]
+                    multiply_row(m, o_t[:, COUT * (m % 2):COUT * (m % 2) + COUT])
+                    if m % 2 == 0:
+                        nc.sync.dma_start(out=out[:, m:m + 2, :].rearrange("n m c -> n (m c)"), in_=o_t[:])
+                else:
+                    o_t = outp.tile([P, 2 * COUT], F32, name="ot%d" % m, tag="ot")
+                    multiply_row(m, o_t[:, 0:COUT])
+                    nc.sync.dma_start(out=out[:, m:m + 1, :].rearrange("n m c -> n (m c)"), in_=o_t[:, 0:COUT])
+
+        transpose_x(3)
+        quantise_w(3, 0)
+        quantise_x(3)
+        transpose_x(2)
+        quantise_w(3, 1)
+        quantise_x(2)
+        rows([15, 14, 13, 12, 11, 10, 9])
+        quantise_w(2, 0)
+        quantise_w(2, 1)
+        transpose_x(1)
+        quantise_x(1)
+        rows([8, 7, 6, 5, 4])
+        quantise_w(1, 0)
+        quantise_w(1, 1)
+        transpose_x(0)
+        quantise_x(0)
+        rows([3, 2, 1])
+        quantise_w(0, 0)
+        quantise_w(0, 1)
+        rows([0])

@@ -9,6 +9,7 @@ U32 = mybir.dt.uint32
 U8 = mybir.dt.uint8
 FP8X4 = mybir.dt.float8_e4m3fn_x4
 COPY = mybir.ActivationFunctionType.Copy
+MULT = mybir.AluOpType.mult
 
 P = 128
 NM = 16
@@ -23,14 +24,14 @@ def tile_linear_pa_kernel(tc, x, weights, path_weights, out):
     with ExitStack() as ctx:
         const = ctx.enter_context(tc.tile_pool(name="const", bufs=1))
         xraw = ctx.enter_context(tc.tile_pool(name="xraw", bufs=1))
-        wraw = ctx.enter_context(tc.tile_pool(name="wraw", bufs=1))
+        big = ctx.enter_context(tc.tile_pool(name="big", bufs=6))
         wgp = ctx.enter_context(tc.tile_pool(name="wgp", bufs=3))
-        wcp = ctx.enter_context(tc.tile_pool(name="wcp", bufs=4))
+        wcp = ctx.enter_context(tc.tile_pool(name="wcp", bufs=6))
         xgp = ctx.enter_context(tc.tile_pool(name="xgp", bufs=2))
         xcp = ctx.enter_context(tc.tile_pool(name="xcp", bufs=1))
-        outp = ctx.enter_context(tc.tile_pool(name="outp", bufs=6))
         psum_t = ctx.enter_context(tc.psum_pool(name="psum_t", bufs=3))
         psum_a = ctx.enter_context(tc.psum_pool(name="psum_a", bufs=5))
+        ctx.enter_context(tc.manual_schedule())
 
         ident = const.tile([P, P], F32)
         make_identity(nc, ident[:])
@@ -39,22 +40,105 @@ def tile_linear_pa_kernel(tc, x, weights, path_weights, out):
         pw_row = const.tile([P, 32], BF16)
         nc.vector.memset(pw_row[:], 0.0)
         nc.scalar.dma_start(out=pw_row[0:1, 0:4], in_=path_weights.unsqueeze(0))
+        pw = const.tile([P, 4], F32)
 
         xr = {}
         wr = {}
+        xg = {}
+        xc = {}
+        xs = {}
+        wg = {}
+        wc = {}
+        ws = {}
 
         def load_x(grp):
-            t = xraw.tile([P, 4 * CIN], BF16, name="xr%d" % grp)
-            nc.sync.dma_start(out=t[:], in_=x[:, 4 * grp:4 * grp + 4, :].rearrange("n m k -> n (m k)"))
-            xr[grp] = t
+            xr[grp] = xraw.tile([P, 4 * CIN], BF16, name="xr%d" % grp)
+            nc.sync.dma_start(out=xr[grp][:], in_=x[:, 4 * grp:4 * grp + 4, :].rearrange("n m k -> n (m k)"))
 
         def load_w(l, g):
-            t = wraw.tile([P, 4 * COUT], BF16, name="wr%d%d" % (l, g))
+            if g == 0:
+                wr[l] = big.tile([P, 8 * COUT], BF16, name="wr%d" % l, tag="big")
             nc.sync.dma_start(
-                out=t[:].rearrange("p (u f) -> p u f", u=2),
-                in_=weights[l, 512 * g:512 * g + 512, :].rearrange("(u p e) n -> p u (e n)", u=2, p=P, e=2),
+                out=wr[l][:, 4 * COUT * g:4 * COUT * (g + 1)],
+                in_=weights[l, 512 * g:512 * g + 512, :].rearrange("(p t) n -> p (t n)", t=4),
             )
-            wr[(l, g)] = t
+
+        def transpose_x(grp):
+            words = xr[grp][:].bitcast(F32).rearrange("n (r g p u) -> n r g u p", r=4, g=2, p=P, u=2)
+            xg[grp] = xgp.tile([P, 4 * CIN], BF16, name="xg%d" % grp, tag="xg", align_bytes=64)
+            g_w = xg[grp][:].bitcast(F32)
+            for r in range(4):
+                xt = psum_t.tile([P, 512], F32, name="xt%d%d" % (grp, r), tag="xt")
+                for g in range(2):
+                    for u in range(2):
+                        j = 2 * g + u
+                        nc.tensor.transpose(xt[:, P * j:P * j + P], words[:, r, g, u, :], ident[:])
+                nc.scalar.copy(
+                    out=g_w[:, 512 * r:512 * r + 512].rearrange("p (g n u) -> p g n u", g=2, u=2),
+                    in_=xt[:].rearrange("p (g u n) -> p g n u", g=2, u=2),
+                )
+
+        def quantise_x(grp):
+            xc[grp] = xcp.tile([P, CIN], U32, name="xc%d" % grp, align_bytes=64)
+            xs[grp] = xcp.tile([P, CIN], U8, name="xs%d" % grp, align_bytes=64)
+            nc.vector.quantize_mx(out=xc[grp][:].bitcast(FP8X4), scales=xs[grp][:], in_=xg[grp][:])
+
+        def regroup_w(l, g):
+            key = (l, g)
+            wg[key] = wgp.tile([P, 4 * COUT], BF16, name="wg%d%d" % key, tag="wg", align_bytes=64)
+            src = wr[l][:, 4 * COUT * g:4 * COUT * (g + 1)].rearrange("p (t n) -> p t n", t=4)
+            for h in range(2):
+                nc.vector.tensor_copy(
+                    out=wg[key][:, 2048 * h:2048 * h + 2048].rearrange("p (c i t) -> p c t i", i=4, t=4),
+                    in_=src[:, :, 512 * h:512 * h + 512].rearrange("p t (c i) -> p c t i", i=4),
+                )
+
+        def quantise_w(l, g):
+            key = (l, g)
+            wc[key] = wcp.tile([P, COUT], U32, name="wc%d%d" % key, tag="wc", align_bytes=64)
+            ws[key] = wcp.tile([P, COUT], U8, name="ws%d%d" % key, tag="ws", align_bytes=64)
+            for h in range(2):
+                nc.vector.quantize_mx(
+                    out=wc[key][:, 512 * h:512 * h + 512].bitcast(FP8X4),
+                    scales=ws[key][:, 512 * h:512 * h + 512],
+                    in_=wg[key][:, 2048 * h:2048 * h + 2048],
+                )
+
+        def multiply_row(m, o_ap, split):
+            l = DEGREE[m]
+            grp = m // 4
+            r = m % 4
+            for h in range(2):
+                acc = psum_a.tile([P, 512], F32, name="acc%d%d" % (m, h), tag="acc")
+                for g in range(2):
+                    s0 = (2 * r + g) * P
+                    nc.tensor.matmul_mx(
+                        out=acc[:],
+                        lhsT=xc[grp][:, s0:s0 + P].bitcast(FP8X4),
+                        lhsT_scale=xs[grp][:, s0:s0 + P],
+                        rhs=wc[(l, g)][:, 512 * h:512 * h + 512].bitcast(FP8X4),
+                        rhs_scale=ws[(l, g)][:, 512 * h:512 * h + 512],
+                        start=(g == 0),
+                        stop=(g == 1),
+                    )
+                if split and h == 1:
+                    nc.vector.tensor_scalar(out=o_ap[:, 512:1024], in0=acc[:], scalar1=pw[:, l:l + 1], scalar2=None, op0=MULT)
+                else:
+                    nc.scalar.activation(out=o_ap[:, 512 * h:512 * h + 512], in_=acc[:], func=COPY, scale=pw[:, l:l + 1])
+
+        ot = {}
+
+        def rows(hi, lo, first, last, split=False):
+            if hi == last:
+                ot[first] = big.tile([P, 4 * COUT], F32, name="ot%d" % first, tag="big")
+            for m in range(hi, lo - 1, -1):
+                multiply_row(m, ot[first][:, COUT * (m - first):COUT * (m - first + 1)], split)
+            if lo == first:
+                n_rows = last - first + 1
+                nc.sync.dma_start(
+                    out=out[:, first:last + 1, :].rearrange("n m c -> n (m c)"),
+                    in_=ot[first][:, 0:COUT * n_rows],
+                )
 
         load_w(3, 0)
         load_x(3)
@@ -69,103 +153,36 @@ def tile_linear_pa_kernel(tc, x, weights, path_weights, out):
         load_w(0, 0)
         load_w(0, 1)
 
+        transpose_x(3)
+        regroup_w(3, 0)
+        quantise_w(3, 0)
+        transpose_x(2)
+        regroup_w(3, 1)
+        quantise_x(3)
+        quantise_w(3, 1)
         pw_ps = psum_t.tile([P, 512], F32, tag="xt")
         nc.tensor.matmul(out=pw_ps[:, 0:32], lhsT=ones[:], rhs=pw_row[:], start=True, stop=True)
-        pw = const.tile([P, 4], F32)
         nc.vector.tensor_copy(out=pw[:], in_=pw_ps[:, 0:4])
-
-        xg = {}
-        xc = {}
-        xs = {}
-        wc = {}
-        ws = {}
-
-        def transpose_x(grp):
-            words = xr[grp][:].bitcast(F32)
-            g_t = xgp.tile([P, 4 * CIN], BF16, name="xg%d" % grp, tag="xg", align_bytes=64)
-            g_w = g_t[:].bitcast(F32)
-            for r in range(4):
-                xt = psum_t.tile([P, 512], F32, tag="xt")
-                for j in range(4):
-                    c0 = 512 * r + 128 * j
-                    nc.tensor.transpose(xt[:, 128 * j:128 * j + 128], words[:, c0:c0 + 128], ident[:])
-                nc.scalar.copy(
-                    out=g_w[:, 512 * r:512 * r + 512].rearrange("p (g n u) -> p g n u", g=2, u=2),
-                    in_=xt[:].rearrange("p (g u n) -> p g n u", g=2, u=2),
-                )
-            xg[grp] = g_t
-
-        def quantise_x(grp):
-            c_t = xcp.tile([P, CIN], U32, name="xc%d" % grp, align_bytes=64)
-            s_t = xcp.tile([P, CIN], U8, name="xs%d" % grp, align_bytes=64)
-            nc.vector.quantize_mx(out=c_t[:].bitcast(FP8X4), scales=s_t[:], in_=xg[grp][:])
-            xc[grp] = c_t
-            xs[grp] = s_t
-
-        def quantise_w(l, g):
-            g_t = wgp.tile([P, 4 * COUT], BF16, name="wg%d%d" % (l, g), tag="wg", align_bytes=64)
-            nc.vector.tensor_copy(
-                out=g_t[:].rearrange("p (c i t) -> p c t i", i=4, t=4),
-                in_=wr[(l, g)][:].rearrange("p (t c i) -> p c t i", t=4, i=4),
-            )
-            c_t = wcp.tile([P, COUT], U32, name="wc%d%d" % (l, g), tag="wc", align_bytes=64)
-            s_t = wcp.tile([P, COUT], U8, name="ws%d%d" % (l, g), tag="ws", align_bytes=64)
-            nc.vector.quantize_mx(out=c_t[:].bitcast(FP8X4), scales=s_t[:], in_=g_t[:])
-            wc[(l, g)] = c_t
-            ws[(l, g)] = s_t
-
-        def multiply_row(m, o_ap):
-            l = DEGREE[m]
-            grp = m // 4
-            r = m % 4
-            for h in range(2):
-                acc = psum_a.tile([P, 512], F32, tag="acc")
-                for g in range(2):
-                    s0 = (2 * r + g) * P
-                    nc.tensor.matmul_mx(
-                        out=acc[:],
-                        lhsT=xc[grp][:, s0:s0 + P].bitcast(FP8X4),
-                        lhsT_scale=xs[grp][:, s0:s0 + P],
-                        rhs=wc[(l, g)][:, 512 * h:512 * h + 512].bitcast(FP8X4),
-                        rhs_scale=ws[(l, g)][:, 512 * h:512 * h + 512],
-                        start=(g == 0),
-                        stop=(g == 1),
-                    )
-                nc.scalar.activation(out=o_ap[:, 512 * h:512 * h + 512], in_=acc[:], func=COPY, scale=pw[:, l:l + 1])
-
-        state = {}
-
-        def rows(ms):
-            for m in ms:
-                if m >= 2:
-                    if m % 2 == 1:
-                        state["ot"] = outp.tile([P, 2 * COUT], F32, name="ot%d" % m, tag="ot")
-                    o_t = state["ot"]
-                    multiply_row(m, o_t[:, COUT * (m % 2):COUT * (m % 2) + COUT])
-                    if m % 2 == 0:
-                        nc.sync.dma_start(out=out[:, m:m + 2, :].rearrange("n m c -> n (m c)"), in_=o_t[:])
-                else:
-                    o_t = outp.tile([P, 2 * COUT], F32, name="ot%d" % m, tag="ot")
-                    multiply_row(m, o_t[:, 0:COUT])
-                    nc.sync.dma_start(out=out[:, m:m + 1, :].rearrange("n m c -> n (m c)"), in_=o_t[:, 0:COUT])
-
-        transpose_x(3)
-        quantise_w(3, 0)
-        quantise_x(3)
-        transpose_x(2)
-        quantise_w(3, 1)
+        rows(15, 12, 12, 15)
+        regroup_w(2, 0)
         quantise_x(2)
-        rows([15, 14, 13, 12, 11, 10, 9])
         quantise_w(2, 0)
-        quantise_w(2, 1)
         transpose_x(1)
+        rows(11, 9, 8, 11)
+        regroup_w(2, 1)
+        quantise_w(2, 1)
+        rows(8, 8, 8, 11)
+        regroup_w(1, 0)
         quantise_x(1)
-        rows([8, 7, 6, 5, 4])
         quantise_w(1, 0)
-        quantise_w(1, 1)
         transpose_x(0)
+        rows(7, 4, 4, 7)
+        regroup_w(1, 1)
         quantise_x(0)
-        rows([3, 2, 1])
+        quantise_w(1, 1)
+        rows(3, 1, 1, 3)
+        regroup_w(0, 0)
         quantise_w(0, 0)
+        regroup_w(0, 1)
         quantise_w(0, 1)
-        rows([0])
+        rows(0, 0, 0, 0, split=True)

@@ -24,8 +24,8 @@ def tile_linear_pa_kernel(tc, x, weights, path_weights, out):
     with ExitStack() as ctx:
         const = ctx.enter_context(tc.tile_pool(name="const", bufs=1))
         xraw = ctx.enter_context(tc.tile_pool(name="xraw", bufs=1))
-        big = ctx.enter_context(tc.tile_pool(name="big", bufs=6))
-        wgp = ctx.enter_context(tc.tile_pool(name="wgp", bufs=3))
+        big = ctx.enter_context(tc.tile_pool(name="big", bufs=7))
+        wgp = ctx.enter_context(tc.tile_pool(name="wgp", bufs=2))
         wcp = ctx.enter_context(tc.tile_pool(name="wcp", bufs=6))
         xgp = ctx.enter_context(tc.tile_pool(name="xgp", bufs=2))
         xcp = ctx.enter_context(tc.tile_pool(name="xcp", bufs=1))
@@ -176,13 +176,15 @@ def tile_linear_pa_kernel(tc, x, weights, path_weights, out):
         quantise_x(1)
         quantise_w(1, 0)
         transpose_x(0)
-        rows(7, 4, 4, 7)
+        rows(7, 6, 6, 7)
+        rows(5, 4, 4, 5)
         regroup_w(1, 1)
         quantise_x(0)
         quantise_w(1, 1)
-        rows(3, 1, 1, 3)
+        rows(3, 2, 2, 3)
+        rows(1, 1, 0, 1)
         regroup_w(0, 0)
         quantise_w(0, 0)
         regroup_w(0, 1)
         quantise_w(0, 1)
-        rows(0, 0, 0, 0, split=True)
+        rows(0, 0, 0, 1, split=True)

@@ -39,7 +39,6 @@ def tile_linear_pa_kernel(tc, x, weights, path_weights, out):
         nc.vector.memset(ones[:], 1.0)
         pw_row = const.tile([P, 32], BF16)
         nc.vector.memset(pw_row[:], 0.0)
-        nc.scalar.dma_start(out=pw_row[0:1, 0:4], in_=path_weights.unsqueeze(0))
         pw = const.tile([P, 4], F32)
 
         xr = {}
@@ -142,6 +141,7 @@ def tile_linear_pa_kernel(tc, x, weights, path_weights, out):
 
         load_w(3, 0)
         load_x(3)
+        nc.sync.dma_start(out=pw_row[0:1, 0:4], in_=path_weights.unsqueeze(0))
         load_w(3, 1)
         load_x(2)
         load_w(2, 0)

@@ -51,12 +51,12 @@ def tile_linear_pa_kernel(tc, x, weights, path_weights, out):
         ws = {}
 
         def load_x(grp):
-            xr[grp] = xraw.tile([P, 4 * CIN], BF16, name="xr%d" % grp)
+            xr[grp] = xraw.tile([P, 4 * CIN], BF16, name="xr%d" % grp, align_bytes=256)
             nc.sync.dma_start(out=xr[grp][:], in_=x[:, 4 * grp:4 * grp + 4, :].rearrange("n m k -> n (m k)"))
 
         def load_w(l, g):
             if g == 0:
-                wr[l] = big.tile([P, 8 * COUT], BF16, name="wr%d" % l, tag="big")
+                wr[l] = big.tile([P, 8 * COUT], BF16, name="wr%d" % l, tag="big", align_bytes=256)
             nc.sync.dma_start(
                 out=wr[l][:, 4 * COUT * g:4 * COUT * (g + 1)],
                 in_=weights[l, 512 * g:512 * g + 512, :].rearrange("(p t) n -> p (t n)", t=4),
@@ -129,7 +129,7 @@ def tile_linear_pa_kernel(tc, x, weights, path_weights, out):
 
         def rows(hi, lo, first, last, split=False):
             if hi == last:
-                ot[first] = big.tile([P, 4 * COUT], F32, name="ot%d" % first, tag="big")
+                ot[first] = big.tile([P, 4 * COUT], F32, name="ot%d" % first, tag="big", align_bytes=256)
             for m in range(hi, lo - 1, -1):
                 multiply_row(m, ot[first][:, COUT * (m - first):COUT * (m - first + 1)], split)
             if lo == first:

@@ -24,7 +24,8 @@ def tile_linear_pa_kernel(tc, x, weights, path_weights, out):
     with ExitStack() as ctx:
         const = ctx.enter_context(tc.tile_pool(name="const", bufs=1))
         xraw = ctx.enter_context(tc.tile_pool(name="xraw", bufs=1))
-        big = ctx.enter_context(tc.tile_pool(name="big", bufs=7))
+        big = ctx.enter_context(tc.tile_pool(name="big", bufs=4))
+        wide = ctx.enter_context(tc.tile_pool(name="wide", bufs=1))
         wgp = ctx.enter_context(tc.tile_pool(name="wgp", bufs=2))
         wcp = ctx.enter_context(tc.tile_pool(name="wcp", bufs=6))
         xgp = ctx.enter_context(tc.tile_pool(name="xgp", bufs=2))
@@ -50,9 +51,12 @@ def tile_linear_pa_kernel(tc, x, weights, path_weights, out):
         wc = {}
         ws = {}
 
-        def load_x(grp):
-            xr[grp] = xraw.tile([P, 4 * CIN], BF16, name="xr%d" % grp, align_bytes=256)
-            nc.sync.dma_start(out=xr[grp][:], in_=x[:, 4 * grp:4 * grp + 4, :].rearrange("n m k -> n (m k)"))
+        def load_x(grp_lo, grp_hi):
+            n_grp = grp_hi - grp_lo + 1
+            raw = xraw.tile([P, 4 * n_grp * CIN], BF16, name="xr%d" % grp_lo, align_bytes=256)
+            nc.sync.dma_start(out=raw[:], in_=x[:, 4 * grp_lo:4 * grp_hi + 4, :].rearrange("n m k -> n (m k)"))
+            for grp in range(grp_lo, grp_hi + 1):
+                xr[grp] = raw[:, 4 * CIN * (grp - grp_lo):4 * CIN * (grp - grp_lo + 1)]
 
         def load_w(l, g):
             if g == 0:
@@ -63,7 +67,7 @@ def tile_linear_pa_kernel(tc, x, weights, path_weights, out):
             )
 
         def transpose_x(grp):
-            words = xr[grp][:].bitcast(F32).rearrange("n (r g p u) -> n r g u p", r=4, g=2, p=P, u=2)
+            words = xr[grp].bitcast(F32).rearrange("n (r g p u) -> n r g u p", r=4, g=2, p=P, u=2)
             xg[grp] = xgp.tile([P, 4 * CIN], BF16, name="xg%d" % grp, tag="xg", align_bytes=64)
             g_w = xg[grp][:].bitcast(F32)
             for r in range(4):
@@ -129,7 +133,11 @@ def tile_linear_pa_kernel(tc, x, weights, path_weights, out):
 
         def rows(hi, lo, first, last, split=False):
             if hi == last:
-                ot[first] = big.tile([P, 4 * COUT], F32, name="ot%d" % first, tag="big", align_bytes=256)
+                n_all = last - first + 1
+                if n_all > 4:
+                    ot[first] = wide.tile([P, n_all * COUT], F32, name="ot%d" % first, align_bytes=256)
+                else:
+                    ot[first] = big.tile([P, n_all * COUT], F32, name="ot%d" % first, tag="big", align_bytes=256)
             for m in range(hi, lo - 1, -1):
                 multiply_row(m, ot[first][:, COUT * (m - first):COUT * (m - first + 1)], split)
             if lo == first:
@@ -140,16 +148,15 @@ def tile_linear_pa_kernel(tc, x, weights, path_weights, out):
                 )
 
         load_w(3, 0)
-        load_x(3)
+        load_x(3, 3)
         nc.sync.dma_start(out=pw_row[0:1, 0:4], in_=path_weights.unsqueeze(0))
         load_w(3, 1)
-        load_x(2)
+        load_x(2, 2)
         load_w(2, 0)
         load_w(2, 1)
-        load_x(1)
+        load_x(0, 1)
         load_w(1, 0)
         load_w(1, 1)
-        load_x(0)
         load_w(0, 0)
         load_w(0, 1)
 
@@ -163,28 +170,26 @@ def tile_linear_pa_kernel(tc, x, weights, path_weights, out):
         pw_ps = psum_t.tile([P, 512], F32, tag="xt")
         nc.tensor.matmul(out=pw_ps[:, 0:32], lhsT=ones[:], rhs=pw_row[:], start=True, stop=True)
         nc.vector.tensor_copy(out=pw[:], in_=pw_ps[:, 0:4])
-        rows(15, 12, 12, 15)
+        rows(15, 12, 9, 15)
         regroup_w(2, 0)
         quantise_x(2)
         quantise_w(2, 0)
+        rows(11, 9, 9, 15)
         transpose_x(1)
-        rows(11, 9, 8, 11)
         regroup_w(2, 1)
         quantise_w(2, 1)
-        rows(8, 8, 8, 11)
+        rows(8, 8, 4, 8)
         regroup_w(1, 0)
         quantise_x(1)
         quantise_w(1, 0)
         transpose_x(0)
-        rows(7, 6, 6, 7)
-        rows(5, 4, 4, 5)
+        rows(7, 4, 4, 8)
         regroup_w(1, 1)
         quantise_x(0)
         quantise_w(1, 1)
-        rows(3, 2, 2, 3)
-        rows(1, 1, 0, 1)
+        rows(3, 1, 1, 3)
         regroup_w(0, 0)
         quantise_w(0, 0)
         regroup_w(0, 1)
         quantise_w(0, 1)
-        rows(0, 0, 0, 1, split=True)
+        rows(0, 0, 0, 0, split=True)

@@ -66,6 +66,13 @@ def tile_linear_pa_kernel(tc, x, weights, path_weights, out):
                 in_=weights[l, 512 * g:512 * g + 512, :].rearrange("(p t) n -> p (t n)", t=4),
             )
 
+        def load_w_whole(l):
+            wr[l] = big.tile([P, 8 * COUT], BF16, name="wr%d" % l, tag="big", align_bytes=256)
+            nc.sync.dma_start(
+                out=wr[l][:].rearrange("p (g c) -> p g c", g=2),
+                in_=weights[l].rearrange("(g p t) n -> p g (t n)", g=2, t=4),
+            )
+
         def transpose_x(grp):
             words = xr[grp].bitcast(F32).rearrange("n (r g p u) -> n r g u p", r=4, g=2, p=P, u=2)
             xg[grp] = xgp.tile([P, 4 * CIN], BF16, name="xg%d" % grp, tag="xg", align_bytes=64)
@@ -157,8 +164,7 @@ def tile_linear_pa_kernel(tc, x, weights, path_weights, out):
         load_x(0, 1)
         load_w(1, 0)
         load_w(1, 1)
-        load_w(0, 0)
-        load_w(0, 1)
+        load_w_whole(0)
 
         transpose_x(3)
         regroup_w(3, 0)

@@ -176,26 +176,27 @@ def tile_linear_pa_kernel(tc, x, weights, path_weights, out):
         pw_ps = psum_t.tile([P, 512], F32, tag="xt")
         nc.tensor.matmul(out=pw_ps[:, 0:32], lhsT=ones[:], rhs=pw_row[:], start=True, stop=True)
         nc.vector.tensor_copy(out=pw[:], in_=pw_ps[:, 0:4])
-        rows(15, 12, 9, 15)
+        rows(15, 12, 8, 15)
         regroup_w(2, 0)
         quantise_x(2)
         quantise_w(2, 0)
-        rows(11, 9, 9, 15)
+        rows(11, 9, 8, 15)
         transpose_x(1)
         regroup_w(2, 1)
         quantise_w(2, 1)
-        rows(8, 8, 4, 8)
+        rows(8, 8, 8, 15)
         regroup_w(1, 0)
         quantise_x(1)
         quantise_w(1, 0)
         transpose_x(0)
-        rows(7, 4, 4, 8)
+        rows(7, 4, 4, 7)
         regroup_w(1, 1)
         quantise_x(0)
         quantise_w(1, 1)
-        rows(3, 1, 1, 3)
+        rows(3, 2, 2, 3)
+        rows(1, 1, 0, 1)
         regroup_w(0, 0)
         quantise_w(0, 0)
         regroup_w(0, 1)
         quantise_w(0, 1)
-        rows(0, 0, 0, 0, split=True)
+        rows(0, 0, 0, 1, split=True)

@@ -53,21 +53,21 @@ def tile_linear_pa_kernel(tc, x, weights, path_weights, out):
 
         def load_x(grp_lo, grp_hi):
             n_grp = grp_hi - grp_lo + 1
-            raw = xraw.tile([P, 4 * n_grp * CIN], BF16, name="xr%d" % grp_lo, align_bytes=256)
+            raw = xraw.tile([P, 4 * n_grp * CIN], BF16, name="xr%d" % grp_lo, align_bytes=4096)
             nc.sync.dma_start(out=raw[:], in_=x[:, 4 * grp_lo:4 * grp_hi + 4, :].rearrange("n m k -> n (m k)"))
             for grp in range(grp_lo, grp_hi + 1):
                 xr[grp] = raw[:, 4 * CIN * (grp - grp_lo):4 * CIN * (grp - grp_lo + 1)]
 
         def load_w(l, g):
             if g == 0:
-                wr[l] = big.tile([P, 8 * COUT], BF16, name="wr%d" % l, tag="big", align_bytes=256)
+                wr[l] = big.tile([P, 8 * COUT], BF16, name="wr%d" % l, tag="big", align_bytes=4096)
             nc.sync.dma_start(
                 out=wr[l][:, 4 * COUT * g:4 * COUT * (g + 1)],
                 in_=weights[l, 512 * g:512 * g + 512, :].rearrange("(p t) n -> p (t n)", t=4),
             )
 
         def load_w_whole(l):
-            wr[l] = big.tile([P, 8 * COUT], BF16, name="wr%d" % l, tag="big", align_bytes=256)
+            wr[l] = big.tile([P, 8 * COUT], BF16, name="wr%d" % l, tag="big", align_bytes=4096)
             nc.sync.dma_start(
                 out=wr[l][:].rearrange("p (g c) -> p g c", g=2),
                 in_=weights[l].rearrange("(g p t) n -> p g (t n)", g=2, t=4),
@@ -142,9 +142,9 @@ def tile_linear_pa_kernel(tc, x, weights, path_weights, out):
             if hi == last:
                 n_all = last - first + 1
                 if n_all > 4:
-                    ot[first] = wide.tile([P, n_all * COUT], F32, name="ot%d" % first, align_bytes=256)
+                    ot[first] = wide.tile([P, n_all * COUT], F32, name="ot%d" % first, align_bytes=4096)
                 else:
-                    ot[first] = big.tile([P, n_all * COUT], F32, name="ot%d" % first, tag="big", align_bytes=256)
+                    ot[first] = big.tile([P, n_all * COUT], F32, name="ot%d" % first, tag="big", align_bytes=4096)
             for m in range(hi, lo - 1, -1):
                 multiply_row(m, ot[first][:, COUT * (m - first):COUT * (m - first + 1)], split)
             if lo == first:

@@ -194,7 +194,7 @@ def tile_linear_pa_kernel(tc, x, weights, path_weights, out):
         quantise_x(0)
         quantise_w(1, 1)
         rows(3, 2, 2, 3)
-        rows(1, 1, 0, 1)
+        rows(1, 1, 0, 1, split=True)
         regroup_w(0, 0)
         quantise_w(0, 0)
         regroup_w(0, 1)

@@ -194,9 +194,9 @@ def tile_linear_pa_kernel(tc, x, weights, path_weights, out):
         quantise_x(0)
         quantise_w(1, 1)
         rows(3, 2, 2, 3)
-        rows(1, 1, 0, 1, split=True)
         regroup_w(0, 0)
         quantise_w(0, 0)
         regroup_w(0, 1)
         quantise_w(0, 1)
+        rows(1, 1, 0, 1, split=True)
         rows(0, 0, 0, 1, split=True)

from contextlib import ExitStack

import concourse.mybir as mybir
from concourse.masks import make_identity

F32 = mybir.dt.float32
BF16 = mybir.dt.bfloat16
U32 = mybir.dt.uint32
U8 = mybir.dt.uint8
FP8X4 = mybir.dt.float8_e4m3fn_x4
COPY = mybir.ActivationFunctionType.Copy
MULT = mybir.AluOpType.mult

P = 128
NM = 16
CIN = 1024
COUT = 1024
FLOPS = 2 * P * NM * CIN * COUT
DEGREE = (0, 1, 1, 1, 2, 2, 2, 2, 2, 3, 3, 3, 3, 3, 3, 3)


def tile_linear_pa_kernel(tc, x, weights, path_weights, out):
    nc = tc.nc
    with ExitStack() as ctx:
        const = ctx.enter_context(tc.tile_pool(name="const", bufs=1))
        xraw = ctx.enter_context(tc.tile_pool(name="xraw", bufs=1))
        big = ctx.enter_context(tc.tile_pool(name="big", bufs=4))
        wide = ctx.enter_context(tc.tile_pool(name="wide", bufs=1))
        wgp = ctx.enter_context(tc.tile_pool(name="wgp", bufs=2))
        wcp = ctx.enter_context(tc.tile_pool(name="wcp", bufs=6))
        xgp = ctx.enter_context(tc.tile_pool(name="xgp", bufs=2))
        xcp = ctx.enter_context(tc.tile_pool(name="xcp", bufs=1))
        psum_t = ctx.enter_context(tc.psum_pool(name="psum_t", bufs=3))
        psum_a = ctx.enter_context(tc.psum_pool(name="psum_a", bufs=5))
        ctx.enter_context(tc.manual_schedule())

        ident = const.tile([P, P], F32)
        make_identity(nc, ident[:])
        ones = const.tile([P, P], BF16)
        nc.vector.memset(ones[:], 1.0)
        pw_row = const.tile([P, 32], BF16)
        nc.vector.memset(pw_row[:], 0.0)
        pw = const.tile([P, 4], F32)

        xr = {}
        wr = {}
        xg = {}
        xc = {}
        xs = {}
        wg = {}
        wc = {}
        ws = {}

        def load_x(grp_lo, grp_hi):
            n_grp = grp_hi - grp_lo + 1
            raw = xraw.tile([P, 4 * n_grp * CIN], BF16, name="xr%d" % grp_lo, align_bytes=4096)
            nc.sync.dma_start(out=raw[:], in_=x[:, 4 * grp_lo:4 * grp_hi + 4, :].rearrange("n m k -> n (m k)"))
            for grp in range(grp_lo, grp_hi + 1):
                xr[grp] = raw[:, 4 * CIN * (grp - grp_lo):4 * CIN * (grp - grp_lo + 1)]

        def load_w(l, g):
            if g == 0:
                wr[l] = big.tile([P, 8 * COUT], BF16, name="wr%d" % l, tag="big", align_bytes=4096)
            nc.sync.dma_start(
                out=wr[l][:, 4 * COUT * g:4 * COUT * (g + 1)],
                in_=weights[l, 512 * g:512 * g + 512, :].rearrange("(p t) n -> p (t n)", t=4),
            )

        def load_w_whole(l):
            wr[l] = big.tile([P, 8 * COUT], BF16, name="wr%d" % l, tag="big", align_bytes=4096)
            nc.sync.dma_start(
                out=wr[l][:].rearrange("p (g c) -> p g c", g=2),
                in_=weights[l].rearrange("(g p t) n -> p g (t n)", g=2, t=4),
            )

        def transpose_x(grp):
            words = xr[grp].bitcast(F32).rearrange("n (r g p u) -> n r g u p", r=4, g=2, p=P, u=2)
            xg[grp] = xgp.tile([P, 4 * CIN], BF16, name="xg%d" % grp, tag="xg", align_bytes=64)
            g_w = xg[grp][:].bitcast(F32)
            for r in range(4):
                xt = psum_t.tile([P, 512], F32, name="xt%d%d" % (grp, r), tag="xt")
                for g in range(2):
                    for u in range(2):
                        j = 2 * g + u
                        nc.tensor.transpose(xt[:, P * j:P * j + P], words[:, r, g, u, :], ident[:])
                nc.scalar.copy(
                    out=g_w[:, 512 * r:512 * r + 512].rearrange("p (g n u) -> p g n u", g=2, u=2),
                    in_=xt[:].rearrange("p (g u n) -> p g n u", g=2, u=2),
                )

        def quantise_x(grp):
            xc[grp] = xcp.tile([P, CIN], U32, name="xc%d" % grp, align_bytes=64)
            xs[grp] = xcp.tile([P, CIN], U8, name="xs%d" % grp, align_bytes=64)
            nc.vector.quantize_mx(out=xc[grp][:].bitcast(FP8X4), scales=xs[grp][:], in_=xg[grp][:])

        def regroup_w(l, g):
            key = (l, g)
            wg[key] = wgp.tile([P, 4 * COUT], BF16, name="wg%d%d" % key, tag="wg", align_bytes=64)
            src = wr[l][:, 4 * COUT * g:4 * COUT * (g + 1)].rearrange("p (t n) -> p t n", t=4)
            for h in range(2):
                nc.vector.tensor_copy(
                    out=wg[key][:, 2048 * h:2048 * h + 2048].rearrange("p (c i t) -> p c t i", i=4, t=4),
                    in_=src[:, :, 512 * h:512 * h + 512].rearrange("p t (c i) -> p c t i", i=4),
                )

        def quantise_w(l, g):
            key = (l, g)
            wc[key] = wcp.tile([P, COUT], U32, name="wc%d%d" % key, tag="wc", align_bytes=64)
            ws[key] = wcp.tile([P, COUT], U8, name="ws%d%d" % key, tag="ws", align_bytes=64)
            for h in range(2):
                nc.vector.quantize_mx(
                    out=wc[key][:, 512 * h:512 * h + 512].bitcast(FP8X4),
                    scales=ws[key][:, 512 * h:512 * h + 512],
                    in_=wg[key][:, 2048 * h:2048 * h + 2048],
                )

        def multiply_row(m, o_ap, split):
            l = DEGREE[m]
            grp = m // 4
            r = m % 4
            for h in range(2):
                acc = psum_a.tile([P, 512], F32, name="acc%d%d" % (m, h), tag="acc")
                for g in range(2):
                    s0 = (2 * r + g) * P
                    nc.tensor.matmul_mx(
                        out=acc[:],
                        lhsT=xc[grp][:, s0:s0 + P].bitcast(FP8X4),
                        lhsT_scale=xs[grp][:, s0:s0 + P],
                        rhs=wc[(l, g)][:, 512 * h:512 * h + 512].bitcast(FP8X4),
                        rhs_scale=ws[(l, g)][:, 512 * h:512 * h + 512],
                        start=(g == 0),
                        stop=(g == 1),
                    )
                if split and h == 1:
                    nc.vector.tensor_scalar(out=o_ap[:, 512:1024], in0=acc[:], scalar1=pw[:, l:l + 1], scalar2=None, op0=MULT)
                else:
                    nc.scalar.activation(out=o_ap[:, 512 * h:512 * h + 512], in_=acc[:], func=COPY, scale=pw[:, l:l + 1])

        ot = {}

        def rows(hi, lo, first, last, split=False):
            if hi == last:
                n_all = last - first + 1
                if n_all > 4:
                    ot[first] = wide.tile([P, n_all * COUT], F32, name="ot%d" % first, align_bytes=4096)
                else:
                    ot[first] = big.tile([P, n_all * COUT], F32, name="ot%d" % first, tag="big", align_bytes=4096)
            for m in range(hi, lo - 1, -1):
                multiply_row(m, ot[first][:, COUT * (m - first):COUT * (m - first + 1)], split)
            if lo == first:
                n_rows = last - first + 1
                nc.sync.dma_start(
                    out=out[:, first:last + 1, :].rearrange("n m c -> n (m c)"),
                    in_=ot[first][:, 0:COUT * n_rows],
                )

        load_w(3, 0)
        load_x(3, 3)
        nc.sync.dma_start(out=pw_row[0:1, 0:4], in_=path_weights.unsqueeze(0))
        load_w(3, 1)
        load_x(2, 2)
        load_w(2, 0)
        load_w(2, 1)
        load_x(0, 1)
        load_w(1, 0)
        load_w(1, 1)
        load_w_whole(0)

        transpose_x(3)
        regroup_w(3, 0)
        quantise_w(3, 0)
        transpose_x(2)
        regroup_w(3, 1)
        quantise_x(3)
        quantise_w(3, 1)
        pw_ps = psum_t.tile([P, 512], F32, tag="xt")
        nc.tensor.matmul(out=pw_ps[:, 0:32], lhsT=ones[:], rhs=pw_row[:], start=True, stop=True)
        nc.vector.tensor_copy(out=pw[:], in_=pw_ps[:, 0:4])
        rows(15, 12, 8, 15)
        regroup_w(2, 0)
        quantise_x(2)
        quantise_w(2, 0)
        rows(11, 9, 8, 15)
        transpose_x(1)
        regroup_w(2, 1)
        quantise_w(2, 1)
        rows(8, 8, 8, 15)
        regroup_w(1, 0)
        quantise_x(1)
        quantise_w(1, 0)
        transpose_x(0)
        rows(7, 4, 4, 7)
        regroup_w(1, 1)
        quantise_x(0)
        quantise_w(1, 1)
        rows(3, 2, 2, 3)
        regroup_w(0, 0)
        quantise_w(0, 0)
        regroup_w(0, 1)
        quantise_w(0, 1)
        rows(1, 1, 0, 1, split=True)
        rows(0, 0, 0, 1, split=True)
